import numpy as np
import ml_dtypes


def mxq(x, axis, fmt="e4m3"):
    dtype, down = {"e4m3": (ml_dtypes.float8_e4m3fn, 7), "e5m2": (ml_dtypes.float8_e5m2, 14)}[fmt]
    v = np.moveaxis(np.asarray(x, np.float32).astype(ml_dtypes.bfloat16).astype(np.float64), axis, -1)
    blocks = v.reshape(v.shape[:-1] + (-1, 32))
    amax = np.abs(blocks).max(-1, keepdims=True)
    byte = np.maximum(np.where(amax > 0, np.frexp(amax)[1] - 1 + 127, 0) - down, 1)
    scale = np.exp2(byte - 127.0)
    codes = (blocks / scale).astype(np.float32).astype(dtype).astype(np.float64)
    return np.moveaxis((codes * scale).reshape(v.shape), -1, axis)


WIDE = False


def mx_kscale(k):
    if not WIDE:
        return np.ones(k)
    levels = np.array([10, -10, 5, -5, 0])
    a = np.random.permutation(np.resize(levels, k // 512 * 4)).reshape(k // 512, 4)
    idx = np.arange(k)
    return np.exp2(a[idx // 512, idx % 128 // 32])


BF16 = ml_dtypes.bfloat16


def bf(x):
    return np.asarray(x, np.float32).astype(BF16)


def f64(x):
    return np.asarray(x).astype(np.float64)


B, H_DIM, W_DIM = 2048, 8, 16
N = H_DIM * W_DIM
INNER = (N + 1) ** 2
EPS = 1e-6
BLK = 32


def setup_inputs():
    lv = np.unique(np.log2(mx_kscale(N * N)))
    lv = lv[np.argsort(-np.abs(lv), kind="stable")]
    t = np.exp2(np.round(np.repeat(np.resize(lv, N // BLK), BLK) / 2))
    f = np.concatenate([np.ones(1), t])
    sc = np.full((N + 1, N + 1), 1.0 / N)
    sc[0, 1:] = 0.4 / np.sqrt(N)
    sc[1:, 0] = 0.4 / np.sqrt(N)
    sc[0, 0] = 0.4
    sc = sc / (f[:, None] * f[None, :])
    return {"x": bf(np.random.standard_normal((B, N)) * t),
            "W": bf(np.random.standard_normal((N, INNER)) * sc.reshape(INNER)),
            "b": bf(np.random.standard_normal(N) * 0.2),
            "gamma": bf(1.0 + 0.1 * np.random.standard_normal(N)),
            "beta": bf(0.1 * np.random.standard_normal(N))}


def reference(x, W, b, gamma, beta):
    x = f64(x)
    W3 = f64(W).reshape(N, N + 1, N + 1)
    p = (x[:, :, None] * x[:, None, :]).reshape(B, N * N)
    vt = np.ascontiguousarray(W3[:, 1:, 1:].reshape(N, N * N).T)
    wa = np.ascontiguousarray(W3[:, 0, 1:].T)
    wb = np.ascontiguousarray(W3[:, 1:, 0].T)
    quad = mxq(p, 1, "e4m3") @ mxq(vt, 0, "e4m3")
    y = quad + x @ wa + x @ wb + W3[:, 0, 0] + f64(b)
    u = np.mean(y, axis=-1, keepdims=True)
    s = np.mean((y - u) ** 2, axis=-1, keepdims=True)
    y = f64(gamma) * (y - u) / np.sqrt(s + EPS) + f64(beta)
    return y.reshape(B, H_DIM, W_DIM)

@@ -1,0 +1,275 @@
+from contextlib import ExitStack
+
+import concourse.mybir as mybir
+from concourse.masks import make_identity
+
+F32 = mybir.dt.float32
+BF16 = mybir.dt.bfloat16
+U32 = mybir.dt.uint32
+U8 = mybir.dt.uint8
+FP8X4 = mybir.dt.float8_e4m3fn_x4
+ALU = mybir.AluOpType
+ACT = mybir.ActivationFunctionType
+
+P = 128
+ROWS = 2048
+NB = ROWS // P
+PASSES = 32
+BANKS = 16
+EPS = 1e-6
+WCOLS = 129 * 129
+FLOPS = 2 * ROWS * 128 * 128 * 128 + 2 * 2 * ROWS * 128 * 128
+
+NV = [10] * NB
+MANUAL = True
+
+
+def ceil16(v):
+    return ((v + 15) // 16) * 16
+
+
+def tile_crossmatrix_kernel(tc, x, W, b, gamma, beta, out):
+    nc = tc.nc
+    out2 = out.rearrange("r h w -> r (h w)")
+    with ExitStack() as ctx:
+        const = ctx.enter_context(tc.tile_pool(name="const", bufs=1))
+        big = ctx.enter_context(tc.tile_pool(name="big", bufs=3))
+        codes = ctx.enter_context(tc.tile_pool(name="codes", bufs=2))
+        stage = ctx.enter_context(tc.tile_pool(name="stage", bufs=2))
+        small = ctx.enter_context(tc.tile_pool(name="small", bufs=3))
+        psum = ctx.enter_context(tc.psum_pool(name="psum", bufs=3))
+        if MANUAL:
+            ctx.enter_context(tc.manual_schedule())
+
+        X2 = const.tile([P, 2048], BF16, name="X2")
+        nc.sync.dma_start(out=X2[:], in_=x.rearrange("(a s) i -> a (s i)", s=16))
+        Wt = big.tile([P, 16656], BF16, tag="prod", name="Wt", align_bytes=64)
+        bounds = [0] + [ceil16((16 * h + 17) * 129) for h in range(7)] + [WCOLS]
+        for h in range(8):
+            nc.sync.dma_start(out=Wt[:, bounds[h]:bounds[h + 1]], in_=W[:, bounds[h]:bounds[h + 1]])
+
+        ident_f = const.tile([P, P], F32, name="ident_f")
+        make_identity(nc, ident_f[:])
+        ident_b = const.tile([P, P], BF16, name="ident_b")
+        make_identity(nc, ident_b[:])
+
+        Zb = const.tile([P, P], BF16, name="Zb")
+        nc.vector.memset(Zb[:], 0.0)
+        E0 = const.tile([P, P], BF16, name="E0")
+        nc.vector.memset(E0[:], 0.0)
+        nc.vector.memset(E0[0:1, :], 1.0)
+        neghalf = const.tile([P, 1], F32, name="neghalf")
+        nc.vector.memset(neghalf[:], -0.5)
+        nc.sync.dma_start(out=Zb[0:1, :], in_=b.rearrange("(o n) -> o n", o=1))
+        g_bf = const.tile([P, P], BF16, name="g_bf")
+        nc.sync.dma_start(out=g_bf[:], in_=gamma.partition_broadcast(P))
+        b_bf = const.tile([P, P], BF16, name="b_bf")
+        nc.sync.dma_start(out=b_bf[:], in_=beta.partition_broadcast(P))
+
+        X2w = X2[:].bitcast(F32)
+        S = const.tile([P, 8, P], F32, name="S")
+        for h in range(2):
+            sp = psum.tile([P, 4, P], F32, tag="xv", name="sp")
+            for u in range(4):
+                k = 4 * h + u
+                nc.tensor.transpose(sp[:, u, :], X2w[:, k * P:(k + 1) * P], ident_f[:])
+            nc.vector.tensor_copy(out=S[:, 4 * h:4 * h + 4, :], in_=sp[:])
+        xTb = const.tile([P, ROWS], BF16, name="xTb")
+        X2v = X2[:].rearrange("a (s i) -> a s i", s=16)
+        xTv = xTb[:].rearrange("j (a s) -> j a s", s=16)
+        for h in range(2):
+            tp = psum.tile([P, 8, P], BF16, tag="xs", name="tp")
+            for u in range(8):
+                nc.tensor.transpose(tp[:, u, :], X2v[:, 8 * h + u, :], ident_b[:])
+            nc.scalar.copy(out=xTv[:, :, 8 * h:8 * h + 8], in_=tp[:].rearrange("j s a -> j a s"))
+        xT4 = const.tile([P, ROWS, 4], BF16, name="xT4")
+        xTf = const.tile([P, ROWS], F32, name="xTf")
+        for blk in range(NB):
+            rows = slice(blk * P, (blk + 1) * P)
+            nc.gpsimd.tensor_scalar(
+                out=xT4[:, rows, :], in0=xTb[:, rows].unsqueeze(2).to_broadcast([P, P, 4]),
+                scalar1=1.0, scalar2=0.0, op0=ALU.mult, op1=ALU.add)
+            nc.gpsimd.tensor_scalar(
+                out=xTf[:, rows], in0=xTb[:, rows],
+                scalar1=1.0, scalar2=0.0, op0=ALU.mult, op1=ALU.add)
+        gam = const.tile([P, P], F32, name="gam")
+        nc.gpsimd.tensor_copy(out=gam[:], in_=g_bf[:])
+        bet = const.tile([P, P], F32, name="bet")
+        nc.gpsimd.tensor_copy(out=bet[:], in_=b_bf[:])
+
+        v_codes = const.tile([P, PASSES * P], U32, name="v_codes", align_bytes=64)
+        v_scales = const.tile([P, PASSES * P], U8, name="v_scales", align_bytes=64)
+        on_vector = (1, 4, 7, 9, 12, 15)
+        pend = []
+
+        def quantise_v(h, vg):
+            nc.vector.quantize_mx(
+                out=v_codes[:, 512 * h:512 * (h + 1)].bitcast(FP8X4),
+                scales=v_scales[:, 512 * h:512 * (h + 1)],
+                in_=vg[:].rearrange("p c o t -> p (c o t)"))
+
+        for h in range(8):
+            vg = stage.tile([P, 4, P, 4], BF16, tag="vg", name="vg", align_bytes=64)
+            for e in range(2):
+                q = 2 * h + e
+                vec = q in on_vector
+                vt = psum.tile([P, 8, P], BF16, tag="xv" if vec else "xs", name="vt")
+                for u in range(8):
+                    col = (8 * q + u + 1) * 129 + 1
+                    nc.tensor.transpose(vt[:, u, :], Wt[:, col:col + P], ident_b[:])
+                src = vt[:].rearrange("p (c t) o -> p c o t", t=4)
+                if vec:
+                    nc.vector.tensor_copy(out=vg[:, 2 * e:2 * e + 2, :, :], in_=src)
+                else:
+                    nc.scalar.copy(out=vg[:, 2 * e:2 * e + 2, :, :], in_=src)
+            pend.append((h, vg))
+            if len(pend) > 1:
+                quantise_v(*pend.pop(0))
+        quantise_v(*pend.pop(0))
+
+        wt = psum.tile([P, 3, P], BF16, tag="xs", name="wt")
+        nc.tensor.transpose(wt[:, 0, :], Wt[:, 0:P], ident_b[:])
+        nc.tensor.transpose(wt[:, 1, :], Wt[:, 1:P + 1], ident_b[:])
+        nc.tensor.transpose(wt[:, 2, :], Wt[:, 129:WCOLS:129], ident_b[:])
+        lw = const.tile([P, 3, P], BF16, name="lw")
+        nc.scalar.copy(out=lw[:], in_=wt[:])
+        lin_sb = const.tile([P, NB, P], F32, name="lin_sb")
+        for h in range(4):
+            lp = psum.tile([P, 4, P], F32, tag="xs", name="lp")
+            for u in range(4):
+                rows = slice((4 * h + u) * P, (4 * h + u + 1) * P)
+                nc.tensor.matmul(lp[:, u, :], lhsT=xTb[:, rows], rhs=lw[:, 1, :], start=True, stop=False)
+                nc.tensor.matmul(lp[:, u, :], lhsT=xTb[:, rows], rhs=lw[:, 2, :], start=False, stop=False)
+                nc.tensor.matmul(lp[:, u, :], lhsT=E0[:], rhs=lw[:, 0, :], start=False, stop=False)
+                nc.tensor.matmul(lp[:, u, :], lhsT=E0[:], rhs=Zb[:], start=False, stop=True)
+            nc.scalar.copy(out=lin_sb[:, 4 * h:4 * h + 4, :], in_=lp[:])
+
+        prods = {}
+        pcs = {}
+        accs = {}
+        pe_hooks = {}
+        v_hooks = {}
+        count = {"vfill": 0, "vtt": 0}
+
+        def prod_of(blk):
+            if blk not in prods:
+                prods[blk] = big.tile([P, PASSES, P, 4], BF16, tag="prod", name="prod", align_bytes=64)
+            return prods[blk]
+
+        def fill(blk, n, tag):
+            t = psum.tile([P, 512], F32, tag=tag, name="xb")
+            a = 8 * blk + n // 2
+            for u in range(4):
+                k = 4 * (n % 2) + u
+                nc.tensor.transpose(t[:, P * u:P * (u + 1)], S[:, k, a:a + 1].to_broadcast([P, P]), ident_f[:])
+            return t
+
+        def quantise(blk, g):
+            if g == 0:
+                pc = codes.tile([P, PASSES * P], U32, tag="pc", name="pc", align_bytes=64)
+                ps = codes.tile([P, PASSES * P], U8, tag="ps", name="ps", align_bytes=64)
+                pcs[blk] = (pc, ps)
+            pc, ps = pcs[blk]
+            nc.vector.quantize_mx(
+                out=pc[:, 1024 * g:1024 * (g + 1)].bitcast(FP8X4),
+                scales=ps[:, 1024 * g:1024 * (g + 1)],
+                in_=prods[blk][:, 8 * g:8 * g + 8, :, :].rearrange("p c r k -> p (c r k)"))
+
+        def mx(blk, g):
+            if g == 0:
+                accs[blk] = psum.tile([P, 512], F32, tag="acc", name="acc", bufs=2)
+            pc, ps = pcs[blk]
+            for c in range(8 * g, 8 * g + 8):
+                cols = slice(P * c, P * (c + 1))
+                nc.tensor.matmul_mx(
+                    out=accs[blk][:, 0:P],
+                    lhsT=pc[:, cols].bitcast(FP8X4), lhsT_scale=ps[:, cols],
+                    rhs=v_codes[:, cols].bitcast(FP8X4), rhs_scale=v_scales[:, cols],
+                    start=(c == 0), stop=(c == PASSES - 1))
+
+        def epilogue(blk):
+            y = small.tile([P, P], F32, tag="y", name="y")
+            nc.vector.tensor_tensor(out=y[:], in0=accs[blk][:, 0:P], in1=lin_sb[:, blk, :], op=ALU.add)
+            st = small.tile([P, 6], F32, tag="st", name="st")
+            nc.vector.bn_stats(out=st[:], in_=y[:])
+            mv = small.tile([P, 2], F32, tag="mv", name="mv")
+            nc.vector.bn_aggr(out=mv[:], in_=st[:])
+            ve = small.tile([P, 1], F32, tag="ve", name="ve")
+            nc.gpsimd.tensor_scalar(out=ve[:], in0=mv[:, 1:2], scalar1=EPS, scalar2=0.0, op0=ALU.add, op1=ALU.add)
+            rs = small.tile([P, 1], F32, tag="rs", name="rs")
+            nc.gpsimd.tensor_tensor(out=rs[:], in0=ve[:], in1=neghalf[:], op=ALU.pow)
+            z = small.tile([P, P], F32, tag="z", name="z")
+            nc.gpsimd.tensor_scalar(out=z[:], in0=y[:], scalar1=mv[:, 0:1], scalar2=rs[:],
+                                    op0=ALU.subtract, op1=ALU.mult)
+            nc.gpsimd.tensor_tensor(out=z[:], in0=z[:], in1=gam[:], op=ALU.mult)
+            nc.gpsimd.tensor_tensor(out=z[:], in0=z[:], in1=bet[:], op=ALU.add)
+            nc.sync.dma_start(out=out2[blk * P:(blk + 1) * P, :], in_=z[:])
+
+        def add_hook(table, key, fn):
+            if key not in table:
+                table[key] = []
+            table[key].append(fn)
+
+        def consume_v(blk, n, t):
+            r0 = 8 * n
+            in1 = t[:].bitcast(BF16).rearrange("p (r c k) -> p c r k", r=8, c=PASSES, k=4)
+            in0 = xT4[:, blk * P + r0:blk * P + r0 + 8, :].unsqueeze(1).to_broadcast([P, PASSES, 8, 4])
+            nc.vector.tensor_tensor(out=prod_of(blk)[:, :, r0:r0 + 8, :], in0=in0, in1=in1, op=ALU.mult)
+            tau = count["vtt"]
+            count["vtt"] = tau + 1
+            nv = NV[blk]
+            if blk >= 1:
+                for g in range(4):
+                    if n == ((g + 1) * nv + 3) // 4 - 1:
+                        quantise(blk - 1, g)
+                        add_hook(pe_hooks, tau + 4, (mx, blk - 1, g))
+                        if g == 3:
+                            add_hook(v_hooks, tau + 6, (epilogue, blk - 1))
+            for fn in v_hooks.pop(tau, []):
+                fn[0](*fn[1:])
+
+        def consume_s(blk, n, t):
+            tb = t[:].bitcast(BF16).rearrange("p (r c k) -> p r c k", r=8, c=PASSES, k=4)
+            for rr in range(8):
+                r = 8 * n + rr
+                nc.scalar.activation(out=prod_of(blk)[:, :, r, :], in_=tb[:, rr, :, :], func=ACT.Copy,
+                                     scale=xTf[:, blk * P + r:blk * P + r + 1])
+
+        order = []
+        for blk in range(NB):
+            nv = NV[blk]
+            ns = BANKS - nv
+            keyed = [((n + 0.5) / nv, 0, blk, n) for n in range(nv)]
+            keyed += [((m + 0.5) / ns, 1, blk, nv + m) for m in range(ns)]
+            order.extend(sorted(keyed))
+
+        vq = []
+        sq = []
+        for item in order:
+            kind, blk, n = item[1], item[2], item[3]
+            if kind == 0:
+                if len(vq) == 3:
+                    consume_v(*vq.pop(0))
+                vq.append((blk, n, fill(blk, n, "xv")))
+                m = count["vfill"]
+                count["vfill"] = m + 1
+                for fn in pe_hooks.pop(m, []):
+                    fn[0](*fn[1:])
+            else:
+                if len(sq) == 3:
+                    consume_s(*sq.pop(0))
+                sq.append((blk, n, fill(blk, n, "xs")))
+        while sq:
+            consume_s(*sq.pop(0))
+        while vq:
+            consume_v(*vq.pop(0))
+        for key in sorted(pe_hooks):
+            for fn in pe_hooks[key]:
+                fn[0](*fn[1:])
+        for key in sorted(v_hooks):
+            for fn in v_hooks[key]:
+                fn[0](*fn[1:])
+        for g in range(4):
+            quantise(NB - 1, g)
+            mx(NB - 1, g)
+        epilogue(NB - 1)

@@ -20,8 +20,79 @@ EPS = 1e-6
 WCOLS = 129 * 129
 FLOPS = 2 * ROWS * 128 * 128 * 128 + 2 * 2 * ROWS * 128 * 128
 
-NV = [10] * NB
+NV = [12] * NB
 MANUAL = True
+
+
+def plan(nv_list, mx_lag=4, epi_lag=6):
+    events = []
+    pe_hooks = {}
+    v_hooks = {}
+    count = {"vfill": 0, "vtt": 0}
+    vq = []
+    sq = []
+
+    def add_hook(table, key, ev):
+        if key not in table:
+            table[key] = []
+        table[key].append(ev)
+
+    def consume_s():
+        blk, n = sq.pop(0)
+        events.append(("act", blk, n))
+
+    def consume_v():
+        blk, n = vq.pop(0)
+        events.append(("tt", blk, n))
+        tau = count["vtt"]
+        count["vtt"] = tau + 1
+        nv = nv_list[blk]
+        if blk >= 1:
+            for g in range(4):
+                if n == ((g + 1) * nv + 3) // 4 - 1:
+                    while sq and sq[0][0] < blk:
+                        consume_s()
+                    events.append(("q", blk - 1, g))
+                    add_hook(pe_hooks, tau + mx_lag, ("mx", blk - 1, g))
+                    if g == 3:
+                        add_hook(v_hooks, tau + epi_lag, ("epi", blk - 1, 0))
+        events.extend(v_hooks.pop(tau, []))
+
+    order = []
+    for blk in range(NB):
+        nv = nv_list[blk]
+        ns = BANKS - nv
+        keyed = [((n + 0.5) / nv, 0, blk, n) for n in range(nv)]
+        keyed += [((m + 0.5) / ns, 1, blk, nv + m) for m in range(ns)]
+        order.extend(sorted(keyed))
+    for item in order:
+        kind, blk, n = item[1], item[2], item[3]
+        if kind == 0:
+            if len(vq) == 3:
+                consume_v()
+            vq.append((blk, n))
+            events.append(("fillv", blk, n))
+            m = count["vfill"]
+            count["vfill"] = m + 1
+            events.extend(pe_hooks.pop(m, []))
+        else:
+            if len(sq) == 3:
+                consume_s()
+            sq.append((blk, n))
+            events.append(("fills", blk, n))
+    while sq:
+        consume_s()
+    while vq:
+        consume_v()
+    for key in sorted(pe_hooks):
+        events.extend(pe_hooks[key])
+    for key in sorted(v_hooks):
+        events.extend(v_hooks[key])
+    for g in range(4):
+        events.append(("q", NB - 1, g))
+        events.append(("mx", NB - 1, g))
+    events.append(("epi", NB - 1, 0))
+    return events
 
 
 def ceil16(v):
@@ -147,9 +218,7 @@ def tile_crossmatrix_kernel(tc, x, W, b, gamma, beta, out):
         prods = {}
         pcs = {}
         accs = {}
-        pe_hooks = {}
-        v_hooks = {}
-        count = {"vfill": 0, "vtt": 0}
+        banks = {}
 
         def prod_of(blk):
             if blk not in prods:
@@ -162,7 +231,7 @@ def tile_crossmatrix_kernel(tc, x, W, b, gamma, beta, out):
             for u in range(4):
                 k = 4 * (n % 2) + u
                 nc.tensor.transpose(t[:, P * u:P * (u + 1)], S[:, k, a:a + 1].to_broadcast([P, P]), ident_f[:])
-            return t
+            banks[(blk, n)] = t
 
         def quantise(blk, g):
             if g == 0:
@@ -205,71 +274,33 @@ def tile_crossmatrix_kernel(tc, x, W, b, gamma, beta, out):
             nc.gpsimd.tensor_tensor(out=z[:], in0=z[:], in1=bet[:], op=ALU.add)
             nc.sync.dma_start(out=out2[blk * P:(blk + 1) * P, :], in_=z[:])
 
-        def add_hook(table, key, fn):
-            if key not in table:
-                table[key] = []
-            table[key].append(fn)
-
-        def consume_v(blk, n, t):
+        def multiply_v(blk, n):
+            t = banks.pop((blk, n))
             r0 = 8 * n
             in1 = t[:].bitcast(BF16).rearrange("p (r c k) -> p c r k", r=8, c=PASSES, k=4)
             in0 = xT4[:, blk * P + r0:blk * P + r0 + 8, :].unsqueeze(1).to_broadcast([P, PASSES, 8, 4])
             nc.vector.tensor_tensor(out=prod_of(blk)[:, :, r0:r0 + 8, :], in0=in0, in1=in1, op=ALU.mult)
-            tau = count["vtt"]
-            count["vtt"] = tau + 1
-            nv = NV[blk]
-            if blk >= 1:
-                for g in range(4):
-                    if n == ((g + 1) * nv + 3) // 4 - 1:
-                        quantise(blk - 1, g)
-                        add_hook(pe_hooks, tau + 4, (mx, blk - 1, g))
-                        if g == 3:
-                            add_hook(v_hooks, tau + 6, (epilogue, blk - 1))
-            for fn in v_hooks.pop(tau, []):
-                fn[0](*fn[1:])
 
-        def consume_s(blk, n, t):
+        def multiply_s(blk, n):
+            t = banks.pop((blk, n))
             tb = t[:].bitcast(BF16).rearrange("p (r c k) -> p r c k", r=8, c=PASSES, k=4)
             for rr in range(8):
                 r = 8 * n + rr
                 nc.scalar.activation(out=prod_of(blk)[:, :, r, :], in_=tb[:, rr, :, :], func=ACT.Copy,
                                      scale=xTf[:, blk * P + r:blk * P + r + 1])
 
-        order = []
-        for blk in range(NB):
-            nv = NV[blk]
-            ns = BANKS - nv
-            keyed = [((n + 0.5) / nv, 0, blk, n) for n in range(nv)]
-            keyed += [((m + 0.5) / ns, 1, blk, nv + m) for m in range(ns)]
-            order.extend(sorted(keyed))
-
-        vq = []
-        sq = []
-        for item in order:
-            kind, blk, n = item[1], item[2], item[3]
-            if kind == 0:
-                if len(vq) == 3:
-                    consume_v(*vq.pop(0))
-                vq.append((blk, n, fill(blk, n, "xv")))
-                m = count["vfill"]
-                count["vfill"] = m + 1
-                for fn in pe_hooks.pop(m, []):
-                    fn[0](*fn[1:])
+        for step, blk, idx in plan(NV):
+            if step == "fillv":
+                fill(blk, idx, "xv")
+            elif step == "fills":
+                fill(blk, idx, "xs")
+            elif step == "tt":
+                multiply_v(blk, idx)
+            elif step == "act":
+                multiply_s(blk, idx)
+            elif step == "q":
+                quantise(blk, idx)
+            elif step == "mx":
+                mx(blk, idx)
             else:
-                if len(sq) == 3:
-                    consume_s(*sq.pop(0))
-                sq.append((blk, n, fill(blk, n, "xs")))
-        while sq:
-            consume_s(*sq.pop(0))
-        while vq:
-            consume_v(*vq.pop(0))
-        for key in sorted(pe_hooks):
-            for fn in pe_hooks[key]:
-                fn[0](*fn[1:])
-        for key in sorted(v_hooks):
-            for fn in v_hooks[key]:
-                fn[0](*fn[1:])
-        for g in range(4):
-            quantise(NB - 1, g)
-            mx(NB - 1, g)
-        epilogue(NB - 1)
+                epilogue(blk)

@@ -16,87 +16,28 @@ ROWS = 2048
 NB = ROWS // P
 PASSES = 32
 BANKS = 16
+SLOTS = NB * BANKS
+GROUPS = 4 * NB
 EPS = 1e-6
 WCOLS = 129 * 129
 FLOPS = 2 * ROWS * 128 * 128 * 128 + 2 * 2 * ROWS * 128 * 128
 
-NV = [12] * NB
-MANUAL = True
+NS = 6
+LAG = 2
+MXLAG = 2
+E1LAG = 4
+E2LAG = 7
 
 
-def plan(nv_list, mx_lag=4, epi_lag=6):
-    events = []
-    pe_hooks = {}
-    v_hooks = {}
-    count = {"vfill": 0, "vtt": 0}
-    vq = []
-    sq = []
-
-    def add_hook(table, key, ev):
-        if key not in table:
-            table[key] = []
-        table[key].append(ev)
-
-    def consume_s():
-        blk, n = sq.pop(0)
-        events.append(("act", blk, n))
-
-    def consume_v():
-        blk, n = vq.pop(0)
-        events.append(("tt", blk, n))
-        tau = count["vtt"]
-        count["vtt"] = tau + 1
-        nv = nv_list[blk]
-        if blk >= 1:
-            for g in range(4):
-                if n == ((g + 1) * nv + 3) // 4 - 1:
-                    while sq and sq[0][0] < blk:
-                        consume_s()
-                    events.append(("q", blk - 1, g))
-                    add_hook(pe_hooks, tau + mx_lag, ("mx", blk - 1, g))
-                    if g == 3:
-                        add_hook(v_hooks, tau + epi_lag, ("epi", blk - 1, 0))
-        events.extend(v_hooks.pop(tau, []))
-
-    order = []
-    for blk in range(NB):
-        nv = nv_list[blk]
-        ns = BANKS - nv
-        keyed = [((n + 0.5) / nv, 0, blk, n) for n in range(nv)]
-        keyed += [((m + 0.5) / ns, 1, blk, nv + m) for m in range(ns)]
-        order.extend(sorted(keyed))
-    for item in order:
-        kind, blk, n = item[1], item[2], item[3]
-        if kind == 0:
-            if len(vq) == 3:
-                consume_v()
-            vq.append((blk, n))
-            events.append(("fillv", blk, n))
-            m = count["vfill"]
-            count["vfill"] = m + 1
-            events.extend(pe_hooks.pop(m, []))
-        else:
-            if len(sq) == 3:
-                consume_s()
-            sq.append((blk, n))
-            events.append(("fills", blk, n))
-    while sq:
-        consume_s()
-    while vq:
-        consume_v()
-    for key in sorted(pe_hooks):
-        events.extend(pe_hooks[key])
-    for key in sorted(v_hooks):
-        events.extend(v_hooks[key])
-    for g in range(4):
-        events.append(("q", NB - 1, g))
-        events.append(("mx", NB - 1, g))
-    events.append(("epi", NB - 1, 0))
-    return events
+def on_scalar(n):
+    return (n * NS) % BANKS < NS
 
 
-def ceil16(v):
-    return ((v + 15) // 16) * 16
+def due(s, first, period, count):
+    k = s - first
+    if k >= 0 and k % period == 0 and k // period < count:
+        return k // period
+    return None
 
 
 def tile_crossmatrix_kernel(tc, x, W, b, gamma, beta, out):
@@ -109,13 +50,12 @@ def tile_crossmatrix_kernel(tc, x, W, b, gamma, beta, out):
         stage = ctx.enter_context(tc.tile_pool(name="stage", bufs=2))
         small = ctx.enter_context(tc.tile_pool(name="small", bufs=3))
         psum = ctx.enter_context(tc.psum_pool(name="psum", bufs=3))
-        if MANUAL:
-            ctx.enter_context(tc.manual_schedule())
+        ctx.enter_context(tc.manual_schedule())
 
         X2 = const.tile([P, 2048], BF16, name="X2")
         nc.sync.dma_start(out=X2[:], in_=x.rearrange("(a s) i -> a (s i)", s=16))
         Wt = big.tile([P, 16656], BF16, tag="prod", name="Wt", align_bytes=64)
-        bounds = [0] + [ceil16((16 * h + 17) * 129) for h in range(7)] + [WCOLS]
+        bounds = [0] + [((16 * h + 17) * 129 + 15) // 16 * 16 for h in range(7)] + [WCOLS]
         for h in range(8):
             nc.sync.dma_start(out=Wt[:, bounds[h]:bounds[h + 1]], in_=W[:, bounds[h]:bounds[h + 1]])
 
@@ -155,7 +95,8 @@ def tile_crossmatrix_kernel(tc, x, W, b, gamma, beta, out):
             nc.scalar.copy(out=xTv[:, :, 8 * h:8 * h + 8], in_=tp[:].rearrange("j s a -> j a s"))
         xT4 = const.tile([P, ROWS, 4], BF16, name="xT4")
         xTf = const.tile([P, ROWS], F32, name="xTf")
-        for blk in range(NB):
+
+        def spread_x(blk):
             rows = slice(blk * P, (blk + 1) * P)
             nc.gpsimd.tensor_scalar(
                 out=xT4[:, rows, :], in0=xTb[:, rows].unsqueeze(2).to_broadcast([P, P, 4]),
@@ -163,6 +104,9 @@ def tile_crossmatrix_kernel(tc, x, W, b, gamma, beta, out):
             nc.gpsimd.tensor_scalar(
                 out=xTf[:, rows], in0=xTb[:, rows],
                 scalar1=1.0, scalar2=0.0, op0=ALU.mult, op1=ALU.add)
+
+        spread_x(0)
+        spread_x(1)
         gam = const.tile([P, P], F32, name="gam")
         nc.gpsimd.tensor_copy(out=gam[:], in_=g_bf[:])
         bet = const.tile([P, P], F32, name="bet")
@@ -170,33 +114,31 @@ def tile_crossmatrix_kernel(tc, x, W, b, gamma, beta, out):
 
         v_codes = const.tile([P, PASSES * P], U32, name="v_codes", align_bytes=64)
         v_scales = const.tile([P, PASSES * P], U8, name="v_scales", align_bytes=64)
-        on_vector = (1, 4, 7, 9, 12, 15)
-        pend = []
+        staged = []
 
-        def quantise_v(h, vg):
+        def quantise_v(h):
             nc.vector.quantize_mx(
                 out=v_codes[:, 512 * h:512 * (h + 1)].bitcast(FP8X4),
                 scales=v_scales[:, 512 * h:512 * (h + 1)],
-                in_=vg[:].rearrange("p c o t -> p (c o t)"))
+                in_=staged[h][:].rearrange("p c o t -> p (c o t)"))
 
         for h in range(8):
             vg = stage.tile([P, 4, P, 4], BF16, tag="vg", name="vg", align_bytes=64)
-            for e in range(2):
-                q = 2 * h + e
-                vec = q in on_vector
-                vt = psum.tile([P, 8, P], BF16, tag="xv" if vec else "xs", name="vt")
-                for u in range(8):
-                    col = (8 * q + u + 1) * 129 + 1
-                    nc.tensor.transpose(vt[:, u, :], Wt[:, col:col + P], ident_b[:])
-                src = vt[:].rearrange("p (c t) o -> p c o t", t=4)
+            staged.append(vg)
+            for e in range(4):
+                c = 4 * h + e
+                vec = c % 3 == 2
+                vt = psum.tile([P, 4, P], BF16, tag="xv" if vec else "xs", name="vt")
+                for t in range(4):
+                    col = (4 * c + t + 1) * 129 + 1
+                    nc.tensor.transpose(vt[:, t, :], Wt[:, col:col + P], ident_b[:])
                 if vec:
-                    nc.vector.tensor_copy(out=vg[:, 2 * e:2 * e + 2, :, :], in_=src)
+                    nc.vector.tensor_copy(out=vg[:, e, :, :], in_=vt[:].rearrange("p t o -> p o t"))
                 else:
-                    nc.scalar.copy(out=vg[:, 2 * e:2 * e + 2, :, :], in_=src)
-            pend.append((h, vg))
-            if len(pend) > 1:
-                quantise_v(*pend.pop(0))
-        quantise_v(*pend.pop(0))
+                    nc.scalar.copy(out=vg[:, e, :, :], in_=vt[:].rearrange("p t o -> p o t"))
+            if h > 0:
+                quantise_v(h - 1)
+        quantise_v(7)
 
         wt = psum.tile([P, 3, P], BF16, tag="xs", name="wt")
         nc.tensor.transpose(wt[:, 0, :], Wt[:, 0:P], ident_b[:])
@@ -204,34 +146,39 @@ def tile_crossmatrix_kernel(tc, x, W, b, gamma, beta, out):
         nc.tensor.transpose(wt[:, 2, :], Wt[:, 129:WCOLS:129], ident_b[:])
         lw = const.tile([P, 3, P], BF16, name="lw")
         nc.scalar.copy(out=lw[:], in_=wt[:])
-        lin_sb = const.tile([P, NB, P], F32, name="lin_sb")
-        for h in range(4):
-            lp = psum.tile([P, 4, P], F32, tag="xs", name="lp")
-            for u in range(4):
-                rows = slice((4 * h + u) * P, (4 * h + u + 1) * P)
-                nc.tensor.matmul(lp[:, u, :], lhsT=xTb[:, rows], rhs=lw[:, 1, :], start=True, stop=False)
-                nc.tensor.matmul(lp[:, u, :], lhsT=xTb[:, rows], rhs=lw[:, 2, :], start=False, stop=False)
-                nc.tensor.matmul(lp[:, u, :], lhsT=E0[:], rhs=lw[:, 0, :], start=False, stop=False)
-                nc.tensor.matmul(lp[:, u, :], lhsT=E0[:], rhs=Zb[:], start=False, stop=True)
-            nc.scalar.copy(out=lin_sb[:, 4 * h:4 * h + 4, :], in_=lp[:])
 
+        banks = {}
         prods = {}
         pcs = {}
         accs = {}
-        banks = {}
+        mids = {}
 
-        def prod_of(blk):
-            if blk not in prods:
-                prods[blk] = big.tile([P, PASSES, P, 4], BF16, tag="prod", name="prod", align_bytes=64)
-            return prods[blk]
-
-        def fill(blk, n, tag):
-            t = psum.tile([P, 512], F32, tag=tag, name="xb")
+        def fill(blk, n):
+            t = psum.tile([P, 512], F32, tag="xs" if on_scalar(n) else "xv", name="xb")
             a = 8 * blk + n // 2
             for u in range(4):
                 k = 4 * (n % 2) + u
                 nc.tensor.transpose(t[:, P * u:P * (u + 1)], S[:, k, a:a + 1].to_broadcast([P, P]), ident_f[:])
             banks[(blk, n)] = t
+
+        def multiply(blk, n):
+            if n == 0:
+                prods[blk] = big.tile([P, PASSES, P, 4], BF16, tag="prod", name="prod", align_bytes=64)
+            prod = prods[blk]
+            xb = banks.pop((blk, n))[:].bitcast(BF16)
+            r0 = 8 * n
+            if on_scalar(n):
+                for rr in range(8):
+                    nc.scalar.activation(
+                        out=prod[:, :, r0 + rr, :],
+                        in_=xb[:, P * rr:P * (rr + 1)].rearrange("p (c k) -> p c k", k=4),
+                        func=ACT.Copy, scale=xTf[:, blk * P + r0 + rr:blk * P + r0 + rr + 1])
+            else:
+                nc.vector.tensor_tensor(
+                    out=prod[:, :, r0:r0 + 8, :],
+                    in0=xT4[:, blk * P + r0:blk * P + r0 + 8, :].unsqueeze(1).to_broadcast([P, PASSES, 8, 4]),
+                    in1=xb.rearrange("p (r c k) -> p c r k", r=8, c=PASSES, k=4),
+                    op=ALU.mult)
 
         def quantise(blk, g):
             if g == 0:
@@ -244,9 +191,15 @@ def tile_crossmatrix_kernel(tc, x, W, b, gamma, beta, out):
                 scales=ps[:, 1024 * g:1024 * (g + 1)],
                 in_=prods[blk][:, 8 * g:8 * g + 8, :, :].rearrange("p c r k -> p (c r k)"))
 
-        def mx(blk, g):
+        def passes(blk, g):
             if g == 0:
-                accs[blk] = psum.tile([P, 512], F32, tag="acc", name="acc", bufs=2)
+                acc = psum.tile([P, 512], F32, tag="acc", name="acc", bufs=2)
+                accs[blk] = acc
+                rows = slice(blk * P, (blk + 1) * P)
+                nc.tensor.matmul(acc[:, P:2 * P], lhsT=xTb[:, rows], rhs=lw[:, 1, :], start=True, stop=False)
+                nc.tensor.matmul(acc[:, P:2 * P], lhsT=xTb[:, rows], rhs=lw[:, 2, :], start=False, stop=False)
+                nc.tensor.matmul(acc[:, P:2 * P], lhsT=E0[:], rhs=lw[:, 0, :], start=False, stop=False)
+                nc.tensor.matmul(acc[:, P:2 * P], lhsT=E0[:], rhs=Zb[:], start=False, stop=True)
             pc, ps = pcs[blk]
             for c in range(8 * g, 8 * g + 8):
                 cols = slice(P * c, P * (c + 1))
@@ -256,51 +209,49 @@ def tile_crossmatrix_kernel(tc, x, W, b, gamma, beta, out):
                     rhs=v_codes[:, cols].bitcast(FP8X4), rhs_scale=v_scales[:, cols],
                     start=(c == 0), stop=(c == PASSES - 1))
 
-        def epilogue(blk):
+        def norm_first(blk, eng):
+            ql = small.tile([P, 2 * P], F32, tag="ql", name="ql")
+            s1 = small.tile([P, 1], F32, tag="s1", name="s1")
+            nc.scalar.activation(out=ql[:], in_=accs[blk][:, 0:2 * P], func=ACT.Copy, accum_out=s1[:])
+            nm = small.tile([P, 1], F32, tag="nm", name="nm")
+            eng.tensor_scalar(out=nm[:], in0=s1[:], scalar1=-1.0 / P, scalar2=0.0, op0=ALU.mult, op1=ALU.add)
             y = small.tile([P, P], F32, tag="y", name="y")
-            nc.vector.tensor_tensor(out=y[:], in0=accs[blk][:, 0:P], in1=lin_sb[:, blk, :], op=ALU.add)
-            st = small.tile([P, 6], F32, tag="st", name="st")
-            nc.vector.bn_stats(out=st[:], in_=y[:])
-            mv = small.tile([P, 2], F32, tag="mv", name="mv")
-            nc.vector.bn_aggr(out=mv[:], in_=st[:])
+            eng.tensor_tensor(out=y[:], in0=ql[:, 0:P], in1=ql[:, P:2 * P], op=ALU.add)
+            mids[blk] = (y, nm)
+
+        def norm_second(blk, eng):
+            y, nm = mids.pop(blk)
+            sq = small.tile([P, P], F32, tag="sq", name="sq")
+            ss = small.tile([P, 1], F32, tag="ss", name="ss")
+            nc.scalar.activation(out=sq[:], in_=y[:], func=ACT.Square, bias=nm[:], accum_out=ss[:])
             ve = small.tile([P, 1], F32, tag="ve", name="ve")
-            nc.gpsimd.tensor_scalar(out=ve[:], in0=mv[:, 1:2], scalar1=EPS, scalar2=0.0, op0=ALU.add, op1=ALU.add)
+            eng.tensor_scalar(out=ve[:], in0=ss[:], scalar1=1.0 / P, scalar2=EPS, op0=ALU.mult, op1=ALU.add)
             rs = small.tile([P, 1], F32, tag="rs", name="rs")
             nc.gpsimd.tensor_tensor(out=rs[:], in0=ve[:], in1=neghalf[:], op=ALU.pow)
             z = small.tile([P, P], F32, tag="z", name="z")
-            nc.gpsimd.tensor_scalar(out=z[:], in0=y[:], scalar1=mv[:, 0:1], scalar2=rs[:],
-                                    op0=ALU.subtract, op1=ALU.mult)
-            nc.gpsimd.tensor_tensor(out=z[:], in0=z[:], in1=gam[:], op=ALU.mult)
-            nc.gpsimd.tensor_tensor(out=z[:], in0=z[:], in1=bet[:], op=ALU.add)
+            eng.tensor_scalar(out=z[:], in0=y[:], scalar1=nm[:], scalar2=rs[:], op0=ALU.add, op1=ALU.mult)
+            eng.tensor_tensor(out=z[:], in0=z[:], in1=gam[:], op=ALU.mult)
+            eng.tensor_tensor(out=z[:], in0=z[:], in1=bet[:], op=ALU.add)
             nc.sync.dma_start(out=out2[blk * P:(blk + 1) * P, :], in_=z[:])
 
-        def multiply_v(blk, n):
-            t = banks.pop((blk, n))
-            r0 = 8 * n
-            in1 = t[:].bitcast(BF16).rearrange("p (r c k) -> p c r k", r=8, c=PASSES, k=4)
-            in0 = xT4[:, blk * P + r0:blk * P + r0 + 8, :].unsqueeze(1).to_broadcast([P, PASSES, 8, 4])
-            nc.vector.tensor_tensor(out=prod_of(blk)[:, :, r0:r0 + 8, :], in0=in0, in1=in1, op=ALU.mult)
-
-        def multiply_s(blk, n):
-            t = banks.pop((blk, n))
-            tb = t[:].bitcast(BF16).rearrange("p (r c k) -> p r c k", r=8, c=PASSES, k=4)
-            for rr in range(8):
-                r = 8 * n + rr
-                nc.scalar.activation(out=prod_of(blk)[:, :, r, :], in_=tb[:, rr, :, :], func=ACT.Copy,
-                                     scale=xTf[:, blk * P + r:blk * P + r + 1])
-
-        for step, blk, idx in plan(NV):
-            if step == "fillv":
-                fill(blk, idx, "xv")
-            elif step == "fills":
-                fill(blk, idx, "xs")
-            elif step == "tt":
-                multiply_v(blk, idx)
-            elif step == "act":
-                multiply_s(blk, idx)
-            elif step == "q":
-                quantise(blk, idx)
-            elif step == "mx":
-                mx(blk, idx)
-            else:
-                epilogue(blk)
+        first_q = BANKS + 3 + LAG
+        last_p = first_q + MXLAG + 12
+        for s in range(SLOTS + last_p - BANKS + E2LAG + 1):
+            if s < SLOTS:
+                fill(s // BANKS, s % BANKS)
+                if s % BANKS == 0 and s // BANKS + 2 < NB:
+                    spread_x(s // BANKS + 2)
+            grp = due(s, first_q + MXLAG, 4, GROUPS)
+            if grp is not None:
+                passes(grp // 4, grp % 4)
+            if LAG <= s < SLOTS + LAG:
+                multiply((s - LAG) // BANKS, (s - LAG) % BANKS)
+            grp = due(s, first_q, 4, GROUPS)
+            if grp is not None:
+                quantise(grp // 4, grp % 4)
+            blk = due(s, last_p + E1LAG, BANKS, NB)
+            if blk is not None:
+                norm_first(blk, nc.vector if blk == NB - 1 else nc.gpsimd)
+            blk = due(s, last_p + E2LAG, BANKS, NB)
+            if blk is not None:
+                norm_second(blk, nc.vector if blk == NB - 1 else nc.gpsimd)

@@ -22,15 +22,18 @@ EPS = 1e-6
 WCOLS = 129 * 129
 FLOPS = 2 * ROWS * 128 * 128 * 128 + 2 * 2 * ROWS * 128 * 128
 
-NS = 6
+def scalar_banks(blk):
+    return 5 if blk % 3 == 0 else 6
+
+
 LAG = 2
 MXLAG = 2
 E1LAG = 4
 E2LAG = 7
 
 
-def on_scalar(n):
-    return (n * NS) % BANKS < NS
+def on_scalar(blk, n):
+    return (n * scalar_banks(blk)) % BANKS < scalar_banks(blk)
 
 
 def due(s, first, period, count):
@@ -154,7 +157,7 @@ def tile_crossmatrix_kernel(tc, x, W, b, gamma, beta, out):
         mids = {}
 
         def fill(blk, n):
-            t = psum.tile([P, 512], F32, tag="xs" if on_scalar(n) else "xv", name="xb")
+            t = psum.tile([P, 512], F32, tag="xs" if on_scalar(blk, n) else "xv", name="xb")
             a = 8 * blk + n // 2
             for u in range(4):
                 k = 4 * (n % 2) + u
@@ -167,7 +170,7 @@ def tile_crossmatrix_kernel(tc, x, W, b, gamma, beta, out):
             prod = prods[blk]
             xb = banks.pop((blk, n))[:].bitcast(BF16)
             r0 = 8 * n
-            if on_scalar(n):
+            if on_scalar(blk, n):
                 for rr in range(8):
                     nc.scalar.activation(
                         out=prod[:, :, r0 + rr, :],

@@ -22,8 +22,17 @@ EPS = 1e-6
 WCOLS = 129 * 129
 FLOPS = 2 * ROWS * 128 * 128 * 128 + 2 * 2 * ROWS * 128 * 128
 
+PE_BANK = 8
+PE_FROM = 1
+PE_AHEAD = 12
+
+
 def scalar_banks(blk):
-    return 5 if blk % 3 == 0 else 6
+    return 5 if blk % 2 else 6
+
+
+def on_tensor(blk, n):
+    return blk >= PE_FROM and n == PE_BANK
 
 
 LAG = 2
@@ -33,7 +42,9 @@ E2LAG = 7
 
 
 def on_scalar(blk, n):
-    return (n * scalar_banks(blk)) % BANKS < scalar_banks(blk)
+    if blk < PE_FROM:
+        return (n * scalar_banks(blk)) % BANKS < scalar_banks(blk)
+    return ((n - (n > PE_BANK)) * scalar_banks(blk)) % (BANKS - 1) < scalar_banks(blk)
 
 
 def due(s, first, period, count):
@@ -79,6 +90,21 @@ def tile_crossmatrix_kernel(tc, x, W, b, gamma, beta, out):
         nc.sync.dma_start(out=g_bf[:], in_=gamma.partition_broadcast(P))
         b_bf = const.tile([P, P], BF16, name="b_bf")
         nc.sync.dma_start(out=b_bf[:], in_=beta.partition_broadcast(P))
+
+        diag = []
+        for i in range(3):
+            rk = const.tile([P, P], BF16, name="rk%d" % i)
+            nc.gpsimd.memset(rk[:], 0.0)
+            dg = const.tile([P, 8, P], BF16, name="dg%d" % i)
+            nc.gpsimd.memset(dg[:].rearrange("p u n -> p (u n)").bitcast(F32), 0.0)
+            diag.append((rk, dg))
+
+        def load_diag(blk):
+            rk, dg = diag[blk % 3]
+            r0 = blk * P + 8 * PE_BANK
+            nc.sync.dma_start(out=rk[0:8, :], in_=x[r0:r0 + 8, :])
+            for u in range(8):
+                nc.sync.dma_start(out=dg[u:u + 1, u, :], in_=x[r0 + u:r0 + u + 1, :])
 
         X2w = X2[:].bitcast(F32)
         S = const.tile([P, 8, P], F32, name="S")
@@ -157,6 +183,15 @@ def tile_crossmatrix_kernel(tc, x, W, b, gamma, beta, out):
         mids = {}
 
         def fill(blk, n):
+            if on_tensor(blk, n):
+                rk, dg = diag[blk % 3]
+                t = psum.tile([P, 8 * P], BF16, tag="xs", name="pb")
+                for h in range(2):
+                    nc.tensor.matmul(
+                        t[:, 4 * P * h:4 * P * (h + 1)], lhsT=rk[:],
+                        rhs=dg[:, 4 * h:4 * h + 4, :].rearrange("p u n -> p (u n)"), start=True, stop=True)
+                banks[(blk, n)] = t
+                return
             t = psum.tile([P, 512], F32, tag="xs" if on_scalar(blk, n) else "xv", name="xb")
             a = 8 * blk + n // 2
             for u in range(4):
@@ -170,7 +205,10 @@ def tile_crossmatrix_kernel(tc, x, W, b, gamma, beta, out):
             prod = prods[blk]
             xb = banks.pop((blk, n))[:].bitcast(BF16)
             r0 = 8 * n
-            if on_scalar(blk, n):
+            if on_tensor(blk, n):
+                nc.scalar.copy(
+                    out=prod[:, :, r0:r0 + 8, :], in_=xb.rearrange("p (r c k) -> p c r k", r=8, c=PASSES, k=4))
+            elif on_scalar(blk, n):
                 for rr in range(8):
                     nc.scalar.activation(
                         out=prod[:, :, r0 + rr, :],
@@ -240,6 +278,9 @@ def tile_crossmatrix_kernel(tc, x, W, b, gamma, beta, out):
         first_q = BANKS + 3 + LAG
         last_p = first_q + MXLAG + 12
         for s in range(SLOTS + last_p - BANKS + E2LAG + 1):
+            a = s + PE_AHEAD
+            if a < SLOTS and on_tensor(a // BANKS, a % BANKS):
+                load_diag(a // BANKS)
             if s < SLOTS:
                 fill(s // BANKS, s % BANKS)
                 if s % BANKS == 0 and s // BANKS + 2 < NB:

@@ -22,29 +22,37 @@ EPS = 1e-6
 WCOLS = 129 * 129
 FLOPS = 2 * ROWS * 128 * 128 * 128 + 2 * 2 * ROWS * 128 * 128
 
-PE_BANK = 8
-PE_FROM = 1
 PE_AHEAD = 12
 
 
+def tensor_banks(blk):
+    if blk == 0:
+        return ()
+    return (4, 12) if blk % 4 == 3 else (8,)
+
+
 def scalar_banks(blk):
-    return 5 if blk % 2 else 6
-
-
-def on_tensor(blk, n):
-    return blk >= PE_FROM and n == PE_BANK
+    if blk == 0:
+        return (9, 13)
+    share = 5
+    rest = [n for n in range(BANKS) if n not in tensor_banks(blk)]
+    return [n for m, n in enumerate(rest) if m * share % len(rest) < share]
 
 
 LAG = 2
 MXLAG = 2
 E1LAG = 4
 E2LAG = 7
+VSTEP = 4
+VLAG = 1
+
+
+def on_tensor(blk, n):
+    return n in tensor_banks(blk)
 
 
 def on_scalar(blk, n):
-    if blk < PE_FROM:
-        return (n * scalar_banks(blk)) % BANKS < scalar_banks(blk)
-    return ((n - (n > PE_BANK)) * scalar_banks(blk)) % (BANKS - 1) < scalar_banks(blk)
+    return n in scalar_banks(blk)
 
 
 def due(s, first, period, count):
@@ -78,14 +86,11 @@ def tile_crossmatrix_kernel(tc, x, W, b, gamma, beta, out):
         ident_b = const.tile([P, P], BF16, name="ident_b")
         make_identity(nc, ident_b[:])
 
-        Zb = const.tile([P, P], BF16, name="Zb")
-        nc.vector.memset(Zb[:], 0.0)
         E0 = const.tile([P, P], BF16, name="E0")
         nc.vector.memset(E0[:], 0.0)
-        nc.vector.memset(E0[0:1, :], 1.0)
+        nc.vector.memset(E0[0:2, :], 1.0)
         neghalf = const.tile([P, 1], F32, name="neghalf")
         nc.vector.memset(neghalf[:], -0.5)
-        nc.sync.dma_start(out=Zb[0:1, :], in_=b.rearrange("(o n) -> o n", o=1))
         g_bf = const.tile([P, P], BF16, name="g_bf")
         nc.sync.dma_start(out=g_bf[:], in_=gamma.partition_broadcast(P))
         b_bf = const.tile([P, P], BF16, name="b_bf")
@@ -98,10 +103,12 @@ def tile_crossmatrix_kernel(tc, x, W, b, gamma, beta, out):
             dg = const.tile([P, 8, P], BF16, name="dg%d" % i)
             nc.gpsimd.memset(dg[:].rearrange("p u n -> p (u n)").bitcast(F32), 0.0)
             diag.append((rk, dg))
+        loaded = []
 
-        def load_diag(blk):
-            rk, dg = diag[blk % 3]
-            r0 = blk * P + 8 * PE_BANK
+        def load_diag(blk, n):
+            rk, dg = diag[len(loaded) % 3]
+            loaded.append((blk, n))
+            r0 = blk * P + 8 * n
             nc.sync.dma_start(out=rk[0:8, :], in_=x[r0:r0 + 8, :])
             for u in range(8):
                 nc.sync.dma_start(out=dg[u:u + 1, u, :], in_=x[r0 + u:r0 + u + 1, :])
@@ -118,10 +125,13 @@ def tile_crossmatrix_kernel(tc, x, W, b, gamma, beta, out):
         X2v = X2[:].rearrange("a (s i) -> a s i", s=16)
         xTv = xTb[:].rearrange("j (a s) -> j a s", s=16)
         for h in range(2):
-            tp = psum.tile([P, 8, P], BF16, tag="xs", name="tp")
+            tp = psum.tile([P, 8, P], BF16, tag="xv" if h else "xs", name="tp")
             for u in range(8):
                 nc.tensor.transpose(tp[:, u, :], X2v[:, 8 * h + u, :], ident_b[:])
-            nc.scalar.copy(out=xTv[:, :, 8 * h:8 * h + 8], in_=tp[:].rearrange("j s a -> j a s"))
+            if h == 0:
+                nc.scalar.copy(out=xTv[:, :, 8 * h:8 * h + 8], in_=tp[:].rearrange("j s a -> j a s"))
+            else:
+                nc.vector.tensor_copy(out=xTv[:, :, 8 * h:8 * h + 8], in_=tp[:].rearrange("j s a -> j a s"))
         xT4 = const.tile([P, ROWS, 4], BF16, name="xT4")
         xTf = const.tile([P, ROWS], F32, name="xTf")
 
@@ -151,30 +161,27 @@ def tile_crossmatrix_kernel(tc, x, W, b, gamma, beta, out):
                 scales=v_scales[:, 512 * h:512 * (h + 1)],
                 in_=staged[h][:].rearrange("p c o t -> p (c o t)"))
 
-        for h in range(8):
-            vg = stage.tile([P, 4, P, 4], BF16, tag="vg", name="vg", align_bytes=64)
-            staged.append(vg)
-            for e in range(4):
-                c = 4 * h + e
-                vec = c % 3 == 2
-                vt = psum.tile([P, 4, P], BF16, tag="xv" if vec else "xs", name="vt")
-                for t in range(4):
-                    col = (4 * c + t + 1) * 129 + 1
-                    nc.tensor.transpose(vt[:, t, :], Wt[:, col:col + P], ident_b[:])
-                if vec:
-                    nc.vector.tensor_copy(out=vg[:, e, :, :], in_=vt[:].rearrange("p t o -> p o t"))
-                else:
-                    nc.scalar.copy(out=vg[:, e, :, :], in_=vt[:].rearrange("p t o -> p o t"))
-            if h > 0:
-                quantise_v(h - 1)
-        quantise_v(7)
+        def turn_v(c):
+            if c % 4 == 0:
+                vg = stage.tile([P, 4, P, 4], BF16, tag="vg", name="vg", align_bytes=64)
+                staged.append(vg)
+            vg = staged[c // 4]
+            tag, depth = ("xs", 3) if c % 2 else ("acc", 2)
+            vt = psum.tile([P, 4, P], BF16, tag=tag, name="vt", bufs=depth)
+            for t in range(4):
+                col = (4 * c + t + 1) * 129 + 1
+                nc.tensor.transpose(vt[:, t, :], Wt[:, col:col + P], ident_b[:])
+            nc.scalar.copy(out=vg[:, c % 4, :, :], in_=vt[:].rearrange("p t o -> p o t"))
 
-        wt = psum.tile([P, 3, P], BF16, tag="xs", name="wt")
-        nc.tensor.transpose(wt[:, 0, :], Wt[:, 0:P], ident_b[:])
-        nc.tensor.transpose(wt[:, 1, :], Wt[:, 1:P + 1], ident_b[:])
-        nc.tensor.transpose(wt[:, 2, :], Wt[:, 129:WCOLS:129], ident_b[:])
         lw = const.tile([P, 3, P], BF16, name="lw")
-        nc.scalar.copy(out=lw[:], in_=wt[:])
+
+        def turn_linear():
+            wt = psum.tile([P, 3, P], BF16, tag="xs", name="wt")
+            nc.tensor.transpose(wt[:, 0, :], Wt[:, 0:P], ident_b[:])
+            nc.tensor.transpose(wt[:, 1, :], Wt[:, 1:P + 1], ident_b[:])
+            nc.tensor.transpose(wt[:, 2, :], Wt[:, 129:WCOLS:129], ident_b[:])
+            nc.scalar.copy(out=lw[:], in_=wt[:])
+            nc.sync.dma_start(out=lw[1:2, 0, :], in_=b.rearrange("(o n) -> o n", o=1))
 
         banks = {}
         prods = {}
@@ -184,7 +191,7 @@ def tile_crossmatrix_kernel(tc, x, W, b, gamma, beta, out):
 
         def fill(blk, n):
             if on_tensor(blk, n):
-                rk, dg = diag[blk % 3]
+                rk, dg = diag[loaded.index((blk, n)) % 3]
                 t = psum.tile([P, 8 * P], BF16, tag="xs", name="pb")
                 for h in range(2):
                     nc.tensor.matmul(
@@ -239,8 +246,7 @@ def tile_crossmatrix_kernel(tc, x, W, b, gamma, beta, out):
                 rows = slice(blk * P, (blk + 1) * P)
                 nc.tensor.matmul(acc[:, P:2 * P], lhsT=xTb[:, rows], rhs=lw[:, 1, :], start=True, stop=False)
                 nc.tensor.matmul(acc[:, P:2 * P], lhsT=xTb[:, rows], rhs=lw[:, 2, :], start=False, stop=False)
-                nc.tensor.matmul(acc[:, P:2 * P], lhsT=E0[:], rhs=lw[:, 0, :], start=False, stop=False)
-                nc.tensor.matmul(acc[:, P:2 * P], lhsT=E0[:], rhs=Zb[:], start=False, stop=True)
+                nc.tensor.matmul(acc[:, P:2 * P], lhsT=E0[:], rhs=lw[:, 0, :], start=False, stop=True)
             pc, ps = pcs[blk]
             for c in range(8 * g, 8 * g + 8):
                 cols = slice(P * c, P * (c + 1))
@@ -280,11 +286,19 @@ def tile_crossmatrix_kernel(tc, x, W, b, gamma, beta, out):
         for s in range(SLOTS + last_p - BANKS + E2LAG + 1):
             a = s + PE_AHEAD
             if a < SLOTS and on_tensor(a // BANKS, a % BANKS):
-                load_diag(a // BANKS)
+                load_diag(a // BANKS, a % BANKS)
             if s < SLOTS:
                 fill(s // BANKS, s % BANKS)
                 if s % BANKS == 0 and s // BANKS + 2 < NB:
                     spread_x(s // BANKS + 2)
+            if s < PASSES // VSTEP:
+                for c in range(VSTEP * s, VSTEP * (s + 1)):
+                    turn_v(c)
+            h = due(s, VLAG + 4 // VSTEP - 1, 4 // VSTEP, 8)
+            if h is not None:
+                quantise_v(h)
+            if s == PASSES // VSTEP:
+                turn_linear()
             grp = due(s, first_q + MXLAG, 4, GROUPS)
             if grp is not None:
                 passes(grp // 4, grp % 4)

from contextlib import ExitStack

import concourse.mybir as mybir
from concourse.masks import make_identity

F32 = mybir.dt.float32
BF16 = mybir.dt.bfloat16
U32 = mybir.dt.uint32
U8 = mybir.dt.uint8
FP8X4 = mybir.dt.float8_e4m3fn_x4
ALU = mybir.AluOpType
ACT = mybir.ActivationFunctionType

P = 128
ROWS = 2048
NB = ROWS // P
PASSES = 32
BANKS = 16
SLOTS = NB * BANKS
GROUPS = 4 * NB
EPS = 1e-6
WCOLS = 129 * 129
FLOPS = 2 * ROWS * 128 * 128 * 128 + 2 * 2 * ROWS * 128 * 128

PE_AHEAD = 12


def tensor_banks(blk):
    if blk == 0:
        return ()
    return (4, 12) if blk % 4 == 3 else (8,)


def scalar_banks(blk):
    if blk == 0:
        return (9, 13)
    share = 5
    rest = [n for n in range(BANKS) if n not in tensor_banks(blk)]
    return [n for m, n in enumerate(rest) if m * share % len(rest) < share]


LAG = 2
MXLAG = 2
E1LAG = 4
E2LAG = 7
VSTEP = 4
VLAG = 1


def on_tensor(blk, n):
    return n in tensor_banks(blk)


def on_scalar(blk, n):
    return n in scalar_banks(blk)


def due(s, first, period, count):
    k = s - first
    if k >= 0 and k % period == 0 and k // period < count:
        return k // period
    return None


def tile_crossmatrix_kernel(tc, x, W, b, gamma, beta, out):
    nc = tc.nc
    out2 = out.rearrange("r h w -> r (h w)")
    with ExitStack() as ctx:
        const = ctx.enter_context(tc.tile_pool(name="const", bufs=1))
        big = ctx.enter_context(tc.tile_pool(name="big", bufs=3))
        codes = ctx.enter_context(tc.tile_pool(name="codes", bufs=2))
        stage = ctx.enter_context(tc.tile_pool(name="stage", bufs=2))
        small = ctx.enter_context(tc.tile_pool(name="small", bufs=3))
        psum = ctx.enter_context(tc.psum_pool(name="psum", bufs=3))
        ctx.enter_context(tc.manual_schedule())

        X2 = const.tile([P, 2048], BF16, name="X2")
        nc.sync.dma_start(out=X2[:], in_=x.rearrange("(a s) i -> a (s i)", s=16))
        Wt = big.tile([P, 16656], BF16, tag="prod", name="Wt", align_bytes=64)
        bounds = [0] + [((16 * h + 17) * 129 + 15) // 16 * 16 for h in range(7)] + [WCOLS]
        for h in range(8):
            nc.sync.dma_start(out=Wt[:, bounds[h]:bounds[h + 1]], in_=W[:, bounds[h]:bounds[h + 1]])

        ident_f = const.tile([P, P], F32, name="ident_f")
        make_identity(nc, ident_f[:])
        ident_b = const.tile([P, P], BF16, name="ident_b")
        make_identity(nc, ident_b[:])

        E0 = const.tile([P, P], BF16, name="E0")
        nc.vector.memset(E0[:], 0.0)
        nc.vector.memset(E0[0:2, :], 1.0)
        neghalf = const.tile([P, 1], F32, name="neghalf")
        nc.vector.memset(neghalf[:], -0.5)
        g_bf = const.tile([P, P], BF16, name="g_bf")
        nc.sync.dma_start(out=g_bf[:], in_=gamma.partition_broadcast(P))
        b_bf = const.tile([P, P], BF16, name="b_bf")
        nc.sync.dma_start(out=b_bf[:], in_=beta.partition_broadcast(P))

        diag = []
        for i in range(3):
            rk = const.tile([P, P], BF16, name="rk%d" % i)
            nc.gpsimd.memset(rk[:], 0.0)
            dg = const.tile([P, 8, P], BF16, name="dg%d" % i)
            nc.gpsimd.memset(dg[:].rearrange("p u n -> p (u n)").bitcast(F32), 0.0)
            diag.append((rk, dg))
        loaded = []

        def load_diag(blk, n):
            rk, dg = diag[len(loaded) % 3]
            loaded.append((blk, n))
            r0 = blk * P + 8 * n
            nc.sync.dma_start(out=rk[0:8, :], in_=x[r0:r0 + 8, :])
            for u in range(8):
                nc.sync.dma_start(out=dg[u:u + 1, u, :], in_=x[r0 + u:r0 + u + 1, :])

        X2w = X2[:].bitcast(F32)
        S = const.tile([P, 8, P], F32, name="S")
        for h in range(2):
            sp = psum.tile([P, 4, P], F32, tag="xv", name="sp")
            for u in range(4):
                k = 4 * h + u
                nc.tensor.transpose(sp[:, u, :], X2w[:, k * P:(k + 1) * P], ident_f[:])
            nc.vector.tensor_copy(out=S[:, 4 * h:4 * h + 4, :], in_=sp[:])
        xTb = const.tile([P, ROWS], BF16, name="xTb")
        X2v = X2[:].rearrange("a (s i) -> a s i", s=16)
        xTv = xTb[:].rearrange("j (a s) -> j a s", s=16)
        for h in range(2):
            tp = psum.tile([P, 8, P], BF16, tag="xv" if h else "xs", name="tp")
            for u in range(8):
                nc.tensor.transpose(tp[:, u, :], X2v[:, 8 * h + u, :], ident_b[:])
            if h == 0:
                nc.scalar.copy(out=xTv[:, :, 8 * h:8 * h + 8], in_=tp[:].rearrange("j s a -> j a s"))
            else:
                nc.vector.tensor_copy(out=xTv[:, :, 8 * h:8 * h + 8], in_=tp[:].rearrange("j s a -> j a s"))
        xT4 = const.tile([P, ROWS, 4], BF16, name="xT4")
        xTf = const.tile([P, ROWS], F32, name="xTf")

        def spread_x(blk):
            rows = slice(blk * P, (blk + 1) * P)
            nc.gpsimd.tensor_scalar(
                out=xT4[:, rows, :], in0=xTb[:, rows].unsqueeze(2).to_broadcast([P, P, 4]),
                scalar1=1.0, scalar2=0.0, op0=ALU.mult, op1=ALU.add)
            nc.gpsimd.tensor_scalar(
                out=xTf[:, rows], in0=xTb[:, rows],
                scalar1=1.0, scalar2=0.0, op0=ALU.mult, op1=ALU.add)

        spread_x(0)
        spread_x(1)
        gam = const.tile([P, P], F32, name="gam")
        nc.gpsimd.tensor_copy(out=gam[:], in_=g_bf[:])
        bet = const.tile([P, P], F32, name="bet")
        nc.gpsimd.tensor_copy(out=bet[:], in_=b_bf[:])

        v_codes = const.tile([P, PASSES * P], U32, name="v_codes", align_bytes=64)
        v_scales = const.tile([P, PASSES * P], U8, name="v_scales", align_bytes=64)
        staged = []

        def quantise_v(h):
            nc.vector.quantize_mx(
                out=v_codes[:, 512 * h:512 * (h + 1)].bitcast(FP8X4),
                scales=v_scales[:, 512 * h:512 * (h + 1)],
                in_=staged[h][:].rearrange("p c o t -> p (c o t)"))

        def turn_v(c):
            if c % 4 == 0:
                vg = stage.tile([P, 4, P, 4], BF16, tag="vg", name="vg", align_bytes=64)
                staged.append(vg)
            vg = staged[c // 4]
            tag, depth = ("xs", 3) if c % 2 else ("acc", 2)
            vt = psum.tile([P, 4, P], BF16, tag=tag, name="vt", bufs=depth)
            for t in range(4):
                col = (4 * c + t + 1) * 129 + 1
                nc.tensor.transpose(vt[:, t, :], Wt[:, col:col + P], ident_b[:])
            nc.scalar.copy(out=vg[:, c % 4, :, :], in_=vt[:].rearrange("p t o -> p o t"))

        lw = const.tile([P, 3, P], BF16, name="lw")

        def turn_linear():
            wt = psum.tile([P, 3, P], BF16, tag="xs", name="wt")
            nc.tensor.transpose(wt[:, 0, :], Wt[:, 0:P], ident_b[:])
            nc.tensor.transpose(wt[:, 1, :], Wt[:, 1:P + 1], ident_b[:])
            nc.tensor.transpose(wt[:, 2, :], Wt[:, 129:WCOLS:129], ident_b[:])
            nc.scalar.copy(out=lw[:], in_=wt[:])
            nc.sync.dma_start(out=lw[1:2, 0, :], in_=b.rearrange("(o n) -> o n", o=1))

        banks = {}
        prods = {}
        pcs = {}
        accs = {}
        mids = {}

        def fill(blk, n):
            if on_tensor(blk, n):
                rk, dg = diag[loaded.index((blk, n)) % 3]
                t = psum.tile([P, 8 * P], BF16, tag="xs", name="pb")
                for h in range(2):
                    nc.tensor.matmul(
                        t[:, 4 * P * h:4 * P * (h + 1)], lhsT=rk[:],
                        rhs=dg[:, 4 * h:4 * h + 4, :].rearrange("p u n -> p (u n)"), start=True, stop=True)
                banks[(blk, n)] = t
                return
            t = psum.tile([P, 512], F32, tag="xs" if on_scalar(blk, n) else "xv", name="xb")
            a = 8 * blk + n // 2
            for u in range(4):
                k = 4 * (n % 2) + u
                nc.tensor.transpose(t[:, P * u:P * (u + 1)], S[:, k, a:a + 1].to_broadcast([P, P]), ident_f[:])
            banks[(blk, n)] = t

        def multiply(blk, n):
            if n == 0:
                prods[blk] = big.tile([P, PASSES, P, 4], BF16, tag="prod", name="prod", align_bytes=64)
            prod = prods[blk]
            xb = banks.pop((blk, n))[:].bitcast(BF16)
            r0 = 8 * n
            if on_tensor(blk, n):
                nc.scalar.copy(
                    out=prod[:, :, r0:r0 + 8, :], in_=xb.rearrange("p (r c k) -> p c r k", r=8, c=PASSES, k=4))
            elif on_scalar(blk, n):
                for rr in range(8):
                    nc.scalar.activation(
                        out=prod[:, :, r0 + rr, :],
                        in_=xb[:, P * rr:P * (rr + 1)].rearrange("p (c k) -> p c k", k=4),
                        func=ACT.Copy, scale=xTf[:, blk * P + r0 + rr:blk * P + r0 + rr + 1])
            else:
                nc.vector.tensor_tensor(
                    out=prod[:, :, r0:r0 + 8, :],
                    in0=xT4[:, blk * P + r0:blk * P + r0 + 8, :].unsqueeze(1).to_broadcast([P, PASSES, 8, 4]),
                    in1=xb.rearrange("p (r c k) -> p c r k", r=8, c=PASSES, k=4),
                    op=ALU.mult)

        def quantise(blk, g):
            if g == 0:
                pc = codes.tile([P, PASSES * P], U32, tag="pc", name="pc", align_bytes=64)
                ps = codes.tile([P, PASSES * P], U8, tag="ps", name="ps", align_bytes=64)
                pcs[blk] = (pc, ps)
            pc, ps = pcs[blk]
            nc.vector.quantize_mx(
                out=pc[:, 1024 * g:1024 * (g + 1)].bitcast(FP8X4),
                scales=ps[:, 1024 * g:1024 * (g + 1)],
                in_=prods[blk][:, 8 * g:8 * g + 8, :, :].rearrange("p c r k -> p (c r k)"))

        def passes(blk, g):
            if g == 0:
                acc = psum.tile([P, 512], F32, tag="acc", name="acc", bufs=2)
                accs[blk] = acc
                rows = slice(blk * P, (blk + 1) * P)
                nc.tensor.matmul(acc[:, P:2 * P], lhsT=xTb[:, rows], rhs=lw[:, 1, :], start=True, stop=False)
                nc.tensor.matmul(acc[:, P:2 * P], lhsT=xTb[:, rows], rhs=lw[:, 2, :], start=False, stop=False)
                nc.tensor.matmul(acc[:, P:2 * P], lhsT=E0[:], rhs=lw[:, 0, :], start=False, stop=True)
            pc, ps = pcs[blk]
            for c in range(8 * g, 8 * g + 8):
                cols = slice(P * c, P * (c + 1))
                nc.tensor.matmul_mx(
                    out=accs[blk][:, 0:P],
                    lhsT=pc[:, cols].bitcast(FP8X4), lhsT_scale=ps[:, cols],
                    rhs=v_codes[:, cols].bitcast(FP8X4), rhs_scale=v_scales[:, cols],
                    start=(c == 0), stop=(c == PASSES - 1))

        def norm_first(blk, eng):
            ql = small.tile([P, 2 * P], F32, tag="ql", name="ql")
            s1 = small.tile([P, 1], F32, tag="s1", name="s1")
            nc.scalar.activation(out=ql[:], in_=accs[blk][:, 0:2 * P], func=ACT.Copy, accum_out=s1[:])
            nm = small.tile([P, 1], F32, tag="nm", name="nm")
            eng.tensor_scalar(out=nm[:], in0=s1[:], scalar1=-1.0 / P, scalar2=0.0, op0=ALU.mult, op1=ALU.add)
            y = small.tile([P, P], F32, tag="y", name="y")
            eng.tensor_tensor(out=y[:], in0=ql[:, 0:P], in1=ql[:, P:2 * P], op=ALU.add)
            mids[blk] = (y, nm)

        def norm_second(blk, eng):
            y, nm = mids.pop(blk)
            sq = small.tile([P, P], F32, tag="sq", name="sq")
            ss = small.tile([P, 1], F32, tag="ss", name="ss")
            nc.scalar.activation(out=sq[:], in_=y[:], func=ACT.Square, bias=nm[:], accum_out=ss[:])
            ve = small.tile([P, 1], F32, tag="ve", name="ve")
            eng.tensor_scalar(out=ve[:], in0=ss[:], scalar1=1.0 / P, scalar2=EPS, op0=ALU.mult, op1=ALU.add)
            rs = small.tile([P, 1], F32, tag="rs", name="rs")
            nc.gpsimd.tensor_tensor(out=rs[:], in0=ve[:], in1=neghalf[:], op=ALU.pow)
            z = small.tile([P, P], F32, tag="z", name="z")
            eng.tensor_scalar(out=z[:], in0=y[:], scalar1=nm[:], scalar2=rs[:], op0=ALU.add, op1=ALU.mult)
            eng.tensor_tensor(out=z[:], in0=z[:], in1=gam[:], op=ALU.mult)
            eng.tensor_tensor(out=z[:], in0=z[:], in1=bet[:], op=ALU.add)
            nc.sync.dma_start(out=out2[blk * P:(blk + 1) * P, :], in_=z[:])

        first_q = BANKS + 3 + LAG
        last_p = first_q + MXLAG + 12
        for s in range(SLOTS + last_p - BANKS + E2LAG + 1):
            a = s + PE_AHEAD
            if a < SLOTS and on_tensor(a // BANKS, a % BANKS):
                load_diag(a // BANKS, a % BANKS)
            if s < SLOTS:
                fill(s // BANKS, s % BANKS)
                if s % BANKS == 0 and s // BANKS + 2 < NB:
                    spread_x(s // BANKS + 2)
            if s < PASSES // VSTEP:
                for c in range(VSTEP * s, VSTEP * (s + 1)):
                    turn_v(c)
            h = due(s, VLAG + 4 // VSTEP - 1, 4 // VSTEP, 8)
            if h is not None:
                quantise_v(h)
            if s == PASSES // VSTEP:
                turn_linear()
            grp = due(s, first_q + MXLAG, 4, GROUPS)
            if grp is not None:
                passes(grp // 4, grp % 4)
            if LAG <= s < SLOTS + LAG:
                multiply((s - LAG) // BANKS, (s - LAG) % BANKS)
            grp = due(s, first_q, 4, GROUPS)
            if grp is not None:
                quantise(grp // 4, grp % 4)
            blk = due(s, last_p + E1LAG, BANKS, NB)
            if blk is not None:
                norm_first(blk, nc.vector if blk == NB - 1 else nc.gpsimd)
            blk = due(s, last_p + E2LAG, BANKS, NB)
            if blk is not None:
                norm_second(blk, nc.vector if blk == NB - 1 else nc.gpsimd)
